import numpy as np
import ml_dtypes


def mxq(x, axis, fmt="e4m3"):
    dtype, down = {"e4m3": (ml_dtypes.float8_e4m3fn, 7), "e5m2": (ml_dtypes.float8_e5m2, 14)}[fmt]
    v = np.moveaxis(np.asarray(x, np.float32).astype(ml_dtypes.bfloat16).astype(np.float64), axis, -1)
    blocks = v.reshape(v.shape[:-1] + (-1, 32))
    amax = np.abs(blocks).max(-1, keepdims=True)
    byte = np.maximum(np.where(amax > 0, np.frexp(amax)[1] - 1 + 127, 0) - down, 1)
    scale = np.exp2(byte - 127.0)
    codes = (blocks / scale).astype(np.float32).astype(dtype).astype(np.float64)
    return np.moveaxis((codes * scale).reshape(v.shape), -1, axis)


WIDE = False


def mx_kscale(k):
    if not WIDE:
        return np.ones(k)
    levels = np.array([10, -10, 5, -5, 0])
    a = np.random.permutation(np.resize(levels, k // 512 * 4)).reshape(k // 512, 4)
    idx = np.arange(k)
    return np.exp2(a[idx // 512, idx % 128 // 32])


BF16 = ml_dtypes.bfloat16


def bf(x):
    return np.asarray(x, np.float32).astype(BF16)


def f64(x):
    return np.asarray(x).astype(np.float64)


B, I, H = 128, 2048, 2048
EPS = 1e-5


def sigmoid(v):
    return 1.0 / (1.0 + np.exp(-v))


def ln(v, g, b):
    m = v.mean(-1, keepdims=True)
    var = np.square(v - m).mean(-1, keepdims=True)
    return (v - m) / np.sqrt(var + EPS) * g + b


def setup_inputs():
    s, t = mx_kscale(I), mx_kscale(H)
    d = {"x": bf(np.random.standard_normal((B, I)) * s), "h": bf(np.random.standard_normal((B, H)) * t),
         "c": bf(np.random.standard_normal((B, H))), "ic_tilde": bf(0.35 * np.random.standard_normal((B, H)))}
    for g in ("f", "o"):
        d["W" + g + "_w"] = bf(np.random.standard_normal((H, I)) / np.sqrt(I) / s[None, :])
        d["W" + g + "_b"] = bf(np.random.standard_normal(H) * 0.5)
        d["U" + g + "_w"] = bf(np.random.standard_normal((H, H)) / np.sqrt(H) / t[None, :])
        d["ln" + g + "_g"] = bf(1.0 + 0.2 * np.random.standard_normal(H))
        d["ln" + g + "_b"] = bf(0.2 * np.random.standard_normal(H))
    return d


def reference(x, h, c, ic_tilde, Wf_w, Wf_b, Uf_w, lnf_g, lnf_b, Wo_w, Wo_b, Uo_w, lno_g, lno_b):
    xq = mxq(f64(x), 1, "e4m3")
    hq = mxq(f64(h), 1, "e4m3")
    pre_f = (xq @ mxq(f64(Wf_w), 1, "e4m3").T) + f64(Wf_b) + (hq @ mxq(f64(Uf_w), 1, "e4m3").T)
    pre_o = (xq @ mxq(f64(Wo_w), 1, "e4m3").T) + f64(Wo_b) + (hq @ mxq(f64(Uo_w), 1, "e4m3").T)
    f = sigmoid(ln(pre_f, f64(lnf_g), f64(lnf_b)))
    o = sigmoid(ln(pre_o, f64(lno_g), f64(lno_b)))
    c_new = f * f64(c) + f64(ic_tilde)
    h_new = o * np.tanh(c_new)
    return (h_new, c_new)

@@ -1,0 +1,276 @@
+from contextlib import ExitStack
+
+import concourse.mybir as mybir
+from concourse.masks import make_identity
+
+F32 = mybir.dt.float32
+BF16 = mybir.dt.bfloat16
+U32 = mybir.dt.uint32
+U8 = mybir.dt.uint8
+FP8X4 = mybir.dt.float8_e4m3fn_x4
+ALU = mybir.AluOpType
+ACT = mybir.ActivationFunctionType
+
+P = 128
+WIDTH = 2048
+K_PASS = 512
+PASSES = WIDTH // K_PASS
+BLOCK = 256
+ROWS_EACH = BLOCK // P
+BANK = 512
+CHUNKS = WIDTH // BANK
+UNITS_PER_GATE = 2 * WIDTH // BLOCK
+UNITS = 2 * UNITS_PER_GATE
+UNITS_PER_BANK = 2 * BANK // BLOCK
+EPS = 1e-5
+
+UNITS_PER_RUN = 2
+LAG = 2
+VECTOR_SHARE = 8
+
+FLOPS = 2 * P * (2 * WIDTH) * (2 * WIDTH)
+
+
+def tile_layernormlstmcell_pb_kernel(
+    tc, x, h, c, ic_tilde, Wf_w, Wf_b, Uf_w, lnf_g, lnf_b, Wo_w, Wo_b, Uo_w, lno_g, lno_b, out_0, out_1
+):
+    nc = tc.nc
+    with ExitStack() as ctx:
+        ctx.enter_context(tc.manual_schedule())
+        keep = ctx.enter_context(tc.tile_pool(name="keep", bufs=1))
+        stage = ctx.enter_context(tc.tile_pool(name="stage", bufs=2))
+        raw_pool = ctx.enter_context(tc.tile_pool(name="raw", bufs=6))
+        grouped_pool = ctx.enter_context(tc.tile_pool(name="grouped", bufs=3))
+        packed_pool = ctx.enter_context(tc.tile_pool(name="packed", bufs=LAG + UNITS_PER_RUN + 1))
+        flip_psum = ctx.enter_context(tc.psum_pool(name="flip", bufs=6))
+        sum_psum = ctx.enter_context(tc.psum_pool(name="sums", bufs=2))
+
+        ident_f32 = keep.tile([P, P], F32)
+        make_identity(nc, ident_f32[:])
+        ident_bf16 = keep.tile([P, P], BF16)
+        make_identity(nc, ident_bf16[:])
+        minus_half = keep.tile([P, 1], F32)
+        nc.vector.memset(minus_half[:], -0.5)
+
+        vectors = {"f_bias": Wf_b, "f_gain": lnf_g, "f_shift": lnf_b, "o_bias": Wo_b, "o_gain": lno_g, "o_shift": lno_b}
+        vector_rows = keep.tile([P, WIDTH], BF16)
+        nc.vector.memset(vector_rows[:], 0.0)
+        for r, name in enumerate(vectors):
+            nc.scalar.dma_start(out=vector_rows[r : r + 1, :], in_=vectors[name].rearrange("(o n) -> o n", o=1))
+        table_warm = keep.tile([P, 1], F32)
+        nc.scalar.activation(out=table_warm[:], in_=minus_half[:], func=ACT.Sigmoid)
+
+        act_codes = {}
+        act_scales = {}
+        for name, source in (("x", x), ("h", h)):
+            act_raw = stage.tile([P, WIDTH], BF16)
+            nc.sync.dma_start(out=act_raw[:], in_=source)
+            act_words = act_raw[:].bitcast(F32)
+            act_grouped = stage.tile([P, PASSES * P * 4], BF16, align_bytes=64)
+            act_grouped_words = act_grouped[:].bitcast(F32)
+            for pair in range(PASSES // 2):
+                flipped = flip_psum.tile([P, 2, 2, P], F32, tag="flip")
+                for g in range(2):
+                    for u in range(2):
+                        first_word = (2 * (2 * pair + g) + u) * P
+                        nc.tensor.transpose(flipped[:, g, u, :], act_words[:, first_word : first_word + P], ident_f32[:])
+                copy_out = nc.scalar.copy if pair == 0 else nc.vector.tensor_copy
+                copy_out(
+                    out=act_grouped_words[:, pair * BANK : (pair + 1) * BANK].rearrange("p (g b u) -> p g b u", g=2, u=2),
+                    in_=flipped[:].rearrange("p g u b -> p g b u"),
+                )
+            act_codes[name] = keep.tile([P, PASSES * P], U32, align_bytes=64, name="codes_" + name)
+            act_scales[name] = keep.tile([P, PASSES * P], U8, align_bytes=64, name="scales_" + name)
+            nc.vector.quantize_mx(out=act_codes[name][:].bitcast(FP8X4), scales=act_scales[name][:], in_=act_grouped[:])
+
+        spread = {}
+        for r, name in enumerate(vectors):
+            spread[name] = keep.tile([P, WIDTH], BF16, name="spread_" + name)
+            for half in range(2):
+                copies = flip_psum.tile([P, 2 * BANK], BF16, tag="flip")
+                for q in range(2):
+                    first = (2 * half + q) * BANK
+                    nc.tensor.matmul(
+                        out=copies[:, q * BANK : (q + 1) * BANK],
+                        lhsT=ident_bf16[:, r : r + 1].to_broadcast([P, P]),
+                        rhs=vector_rows[:, first : first + BANK],
+                        start=True,
+                        stop=True,
+                    )
+                copy_out = nc.scalar.copy if half == 0 else nc.vector.tensor_copy
+                copy_out(out=spread[name][:, half * 2 * BANK : (half + 1) * 2 * BANK], in_=copies[:])
+
+        pre = {}
+        normed = {}
+        gate = {}
+        stats = {}
+        mean_var = {}
+        var_eps = {}
+        rstd = {}
+        for a in ("f", "o"):
+            pre[a] = keep.tile([P, WIDTH], F32, name="pre_" + a)
+            normed[a] = keep.tile([P, WIDTH], F32, name="normed_" + a)
+            gate[a] = keep.tile([P, WIDTH], F32, name="gate_" + a)
+            stats[a] = keep.tile([P, CHUNKS, 6], F32, name="stats_" + a)
+            mean_var[a] = keep.tile([P, 2], F32, name="mean_var_" + a)
+            var_eps[a] = keep.tile([P, 1], F32, name="var_eps_" + a)
+            rstd[a] = keep.tile([P, 1], F32, name="rstd_" + a)
+        c_old = keep.tile([P, WIDTH], BF16)
+        ic_in = keep.tile([P, WIDTH], BF16)
+        c_new = keep.tile([P, WIDTH], F32)
+        tanh_c = keep.tile([P, WIDTH], F32)
+        h_new = keep.tile([P, WIDTH], F32)
+
+        def chunk_columns(chunk):
+            return slice(chunk * BANK, (chunk + 1) * BANK)
+
+        def centre_and_gain(a, cols):
+            nc.vector.scalar_tensor_tensor(
+                out=normed[a][:, cols], in0=pre[a][:, cols], scalar=mean_var[a][:, 0:1],
+                in1=spread[a + "_gain"][:, cols], op0=ALU.subtract, op1=ALU.mult,
+            )
+
+        def scale_and_shift(a, cols):
+            nc.vector.scalar_tensor_tensor(
+                out=normed[a][:, cols], in0=normed[a][:, cols], scalar=rstd[a][:, 0:1],
+                in1=spread[a + "_shift"][:, cols], op0=ALU.mult, op1=ALU.add,
+            )
+
+        def squash(a, cols):
+            nc.scalar.activation(out=gate[a][:, cols], in_=normed[a][:, cols], func=ACT.Sigmoid)
+
+        weights = {"f": (Wf_w, Uf_w), "o": (Wo_w, Uo_w)}
+        raw_of = {}
+        grouped_of = {}
+        codes_of = {}
+        scales_of = {}
+        sums_of = {}
+
+        def load(i):
+            a = "f" if i < UNITS_PER_GATE else "o"
+            block, which = divmod(i % UNITS_PER_GATE, 2)
+            rows = weights[a][which][block * BLOCK : (block + 1) * BLOCK, :]
+            raw_of[i] = raw_pool.tile([P, ROWS_EACH, WIDTH], BF16, name="raw", tag="raw")
+            nc.sync.dma_start(out=raw_of[i][:], in_=rows.rearrange("(j s) k -> j s k", s=ROWS_EACH))
+
+        def transpose_and_copy(i):
+            raw_words = raw_of[i][:].bitcast(F32)
+            grouped_of[i] = grouped_pool.tile([P, PASSES * BLOCK * 4], BF16, align_bytes=64, name="grouped", tag="grouped")
+            grouped_words = grouped_of[i][:].bitcast(F32)
+            for g in range(PASSES):
+                flipped = flip_psum.tile([P, 2, BLOCK], F32, tag="flip")
+                for u in range(2):
+                    for s in range(ROWS_EACH):
+                        first_word = (2 * g + u) * P
+                        nc.tensor.transpose(
+                            flipped[:, u, s * P : (s + 1) * P], raw_words[:, s, first_word : first_word + P], ident_f32[:]
+                        )
+                to_vector = (PASSES * i + g) % VECTOR_SHARE == VECTOR_SHARE - 1
+                copy_out = nc.vector.tensor_copy if to_vector else nc.scalar.copy
+                copy_out(
+                    out=grouped_words[:, g * BANK : (g + 1) * BANK].rearrange("p (n u) -> p n u", u=2),
+                    in_=flipped[:].rearrange("p u n -> p n u"),
+                )
+
+        def quantise(i):
+            codes_of[i] = packed_pool.tile([P, PASSES * BLOCK], U32, align_bytes=64, name="codes", tag="codes")
+            scales_of[i] = packed_pool.tile([P, PASSES * BLOCK], U8, align_bytes=64, name="scales", tag="scales")
+            for half in range(2):
+                words = slice(half * 2 * BLOCK, (half + 1) * 2 * BLOCK)
+                nc.vector.quantize_mx(
+                    out=codes_of[i][:, words].bitcast(FP8X4),
+                    scales=scales_of[i][:, words],
+                    in_=grouped_of[i][:, half * 8 * BLOCK : (half + 1) * 8 * BLOCK],
+                )
+
+        def multiply(i):
+            bank_number, place = divmod(i, UNITS_PER_BANK)
+            block_in_bank, which = divmod(place, 2)
+            if place == 0:
+                sums_of[bank_number] = sum_psum.tile([P, BANK], F32, name="sums", tag="sums")
+            name = "x" if which == 0 else "h"
+            for g in range(PASSES):
+                nc.tensor.matmul_mx(
+                    out=sums_of[bank_number][:, block_in_bank * BLOCK : (block_in_bank + 1) * BLOCK],
+                    lhsT=act_codes[name][:, g * P : (g + 1) * P].bitcast(FP8X4),
+                    lhsT_scale=act_scales[name][:, g * P : (g + 1) * P],
+                    rhs=codes_of[i][:, g * BLOCK : (g + 1) * BLOCK].bitcast(FP8X4),
+                    rhs_scale=scales_of[i][:, g * BLOCK : (g + 1) * BLOCK],
+                    start=(which == 0 and g == 0),
+                    stop=(which == 1 and g == PASSES - 1),
+                )
+
+        def add_bias_and_count(bank_number):
+            a = "f" if bank_number < CHUNKS else "o"
+            chunk = bank_number % CHUNKS
+            cols = chunk_columns(chunk)
+            nc.vector.tensor_tensor(
+                out=pre[a][:, cols].rearrange("p (b j s) -> p b j s", b=2, s=ROWS_EACH),
+                in0=sums_of[bank_number][:].rearrange("p (b s j) -> p b j s", b=2, s=ROWS_EACH),
+                in1=spread[a + "_bias"][:, cols].rearrange("p (b j s) -> p b j s", b=2, s=ROWS_EACH),
+                op=ALU.add,
+            )
+            nc.vector.bn_stats(out=stats[a][:, chunk, :], in_=pre[a][:, cols])
+
+        def mean_and_rstd(a):
+            nc.vector.bn_aggr(out=mean_var[a][:], in_=stats[a][:].rearrange("p n six -> p (n six)"))
+            nc.vector.tensor_scalar_add(out=var_eps[a][:], in0=mean_var[a][:, 1:2], scalar1=EPS)
+            nc.gpsimd.tensor_tensor(out=rstd[a][:], in0=var_eps[a][:], in1=minus_half[:], op=ALU.pow)
+
+        def forget_step_on_vector(step_number):
+            chunk, step = divmod(step_number, 4)
+            cols = chunk_columns(chunk)
+            if step == 0:
+                centre_and_gain("f", cols)
+            if step == 1:
+                scale_and_shift("f", cols)
+            if step == 2:
+                nc.vector.tensor_mul(out=c_new[:, cols], in0=gate["f"][:, cols], in1=c_old[:, cols])
+            if step == 3:
+                nc.vector.tensor_add(out=c_new[:, cols], in0=c_new[:, cols], in1=ic_in[:, cols])
+
+        def forget_step_on_scalar(step_number):
+            chunk, step = divmod(step_number, 4)
+            cols = chunk_columns(chunk)
+            if step == 1:
+                squash("f", cols)
+            if step == 3:
+                nc.scalar.activation(out=tanh_c[:, cols], in_=c_new[:, cols], func=ACT.Tanh)
+
+        first_forget_step = UNITS_PER_GATE + LAG
+        for run_start in range(0, UNITS + LAG, UNITS_PER_RUN):
+            run = range(run_start, run_start + UNITS_PER_RUN)
+            for i in run:
+                if i == UNITS_PER_GATE:
+                    nc.sync.dma_start(out=c_old[:], in_=c)
+                    nc.sync.dma_start(out=ic_in[:], in_=ic_tilde)
+                if i < UNITS:
+                    load(i)
+                if 1 <= i <= UNITS:
+                    quantise(i - 1)
+                if i >= first_forget_step:
+                    forget_step_on_vector(i - first_forget_step)
+                if i < UNITS:
+                    transpose_and_copy(i)
+                if i >= first_forget_step:
+                    forget_step_on_scalar(i - first_forget_step)
+            for i in run:
+                if i >= LAG:
+                    multiply(i - LAG)
+                    if (i - LAG) % UNITS_PER_BANK == UNITS_PER_BANK - 1:
+                        add_bias_and_count((i - LAG) // UNITS_PER_BANK)
+                    if i - LAG == UNITS_PER_GATE - 1:
+                        mean_and_rstd("f")
+
+        nc.sync.dma_start(out=out_1, in_=c_new[:])
+
+        mean_and_rstd("o")
+        for chunk in range(CHUNKS):
+            centre_and_gain("o", chunk_columns(chunk))
+        for chunk in range(CHUNKS):
+            scale_and_shift("o", chunk_columns(chunk))
+            squash("o", chunk_columns(chunk))
+        for chunk in range(CHUNKS):
+            cols = chunk_columns(chunk)
+            nc.vector.tensor_mul(out=h_new[:, cols], in0=gate["o"][:, cols], in1=tanh_c[:, cols])
+            nc.sync.dma_start(out=out_0[:, cols], in_=h_new[:, cols])

@@ -7,6 +7,7 @@ F32 = mybir.dt.float32
 BF16 = mybir.dt.bfloat16
 U32 = mybir.dt.uint32
 U8 = mybir.dt.uint8
+I32 = mybir.dt.int32
 FP8X4 = mybir.dt.float8_e4m3fn_x4
 ALU = mybir.AluOpType
 ACT = mybir.ActivationFunctionType
@@ -27,6 +28,7 @@ EPS = 1e-5
 UNITS_PER_RUN = 2
 LAG = 2
 VECTOR_SHARE = 8
+PREFETCH = 3
 
 FLOPS = 2 * P * (2 * WIDTH) * (2 * WIDTH)
 
@@ -53,38 +55,22 @@ def tile_layernormlstmcell_pb_kernel(
         nc.vector.memset(minus_half[:], -0.5)
 
         vectors = {"f_bias": Wf_b, "f_gain": lnf_g, "f_shift": lnf_b, "o_bias": Wo_b, "o_gain": lno_g, "o_shift": lno_b}
+        vector_names = list(vectors)
         vector_rows = keep.tile([P, WIDTH], BF16)
-        nc.vector.memset(vector_rows[:], 0.0)
-        for r, name in enumerate(vectors):
-            nc.scalar.dma_start(out=vector_rows[r : r + 1, :], in_=vectors[name].rearrange("(o n) -> o n", o=1))
+        nc.vector.memset(vector_rows[:].bitcast(I32), 0)
+
+        def load_vector(queue, r):
+            queue.dma_start(out=vector_rows[r : r + 1, :], in_=vectors[vector_names[r]].rearrange("(o n) -> o n", o=1))
+
+        for r in range(3):
+            load_vector(nc.scalar, r)
         table_warm = keep.tile([P, 1], F32)
         nc.scalar.activation(out=table_warm[:], in_=minus_half[:], func=ACT.Sigmoid)
 
-        act_codes = {}
-        act_scales = {}
-        for name, source in (("x", x), ("h", h)):
-            act_raw = stage.tile([P, WIDTH], BF16)
-            nc.sync.dma_start(out=act_raw[:], in_=source)
-            act_words = act_raw[:].bitcast(F32)
-            act_grouped = stage.tile([P, PASSES * P * 4], BF16, align_bytes=64)
-            act_grouped_words = act_grouped[:].bitcast(F32)
-            for pair in range(PASSES // 2):
-                flipped = flip_psum.tile([P, 2, 2, P], F32, tag="flip")
-                for g in range(2):
-                    for u in range(2):
-                        first_word = (2 * (2 * pair + g) + u) * P
-                        nc.tensor.transpose(flipped[:, g, u, :], act_words[:, first_word : first_word + P], ident_f32[:])
-                copy_out = nc.scalar.copy if pair == 0 else nc.vector.tensor_copy
-                copy_out(
-                    out=act_grouped_words[:, pair * BANK : (pair + 1) * BANK].rearrange("p (g b u) -> p g b u", g=2, u=2),
-                    in_=flipped[:].rearrange("p g u b -> p g b u"),
-                )
-            act_codes[name] = keep.tile([P, PASSES * P], U32, align_bytes=64, name="codes_" + name)
-            act_scales[name] = keep.tile([P, PASSES * P], U8, align_bytes=64, name="scales_" + name)
-            nc.vector.quantize_mx(out=act_codes[name][:].bitcast(FP8X4), scales=act_scales[name][:], in_=act_grouped[:])
-
         spread = {}
-        for r, name in enumerate(vectors):
+
+        def spread_vector(r):
+            name = vector_names[r]
             spread[name] = keep.tile([P, WIDTH], BF16, name="spread_" + name)
             for half in range(2):
                 copies = flip_psum.tile([P, 2 * BANK], BF16, tag="flip")
@@ -99,6 +85,46 @@ def tile_layernormlstmcell_pb_kernel(
                     )
                 copy_out = nc.scalar.copy if half == 0 else nc.vector.tensor_copy
                 copy_out(out=spread[name][:, half * 2 * BANK : (half + 1) * 2 * BANK], in_=copies[:])
+
+        weights = {"f": (Wf_w, Uf_w), "o": (Wo_w, Uo_w)}
+        raw_of = {}
+
+        def load(i):
+            a = "f" if i < UNITS_PER_GATE else "o"
+            block, which = divmod(i % UNITS_PER_GATE, 2)
+            rows = weights[a][which][block * BLOCK : (block + 1) * BLOCK, :]
+            raw_of[i] = raw_pool.tile([P, ROWS_EACH, WIDTH], BF16, name="raw", tag="raw")
+            nc.sync.dma_start(out=raw_of[i][:], in_=rows.rearrange("(j s) k -> j s k", s=ROWS_EACH))
+
+        act_raw = {}
+        for name, source in (("x", x), ("h", h)):
+            act_raw[name] = keep.tile([P, WIDTH], BF16, name="raw_" + name)
+            nc.sync.dma_start(out=act_raw[name][:], in_=source)
+        for i in range(PREFETCH):
+            load(i)
+
+        act_codes = {}
+        act_scales = {}
+        for name in ("x", "h"):
+            act_words = act_raw[name][:].bitcast(F32)
+            act_grouped = stage.tile([P, PASSES * P * 4], BF16, align_bytes=64)
+            act_grouped_words = act_grouped[:].bitcast(F32)
+            for pair in range(PASSES // 2):
+                flipped = flip_psum.tile([P, 2, 2, P], F32, tag="flip")
+                for g in (2 * pair, 2 * pair + 1):
+                    for u in range(2):
+                        first_word = (2 * g + u) * P
+                        nc.tensor.transpose(flipped[:, g % 2, u, :], act_words[:, first_word : first_word + P], ident_f32[:])
+                copy_out = nc.scalar.copy if pair == 0 else nc.vector.tensor_copy
+                copy_out(
+                    out=act_grouped_words[:, pair * BANK : (pair + 1) * BANK].rearrange("p (g b u) -> p g b u", g=2, u=2),
+                    in_=flipped[:].rearrange("p g u b -> p g b u"),
+                )
+            act_codes[name] = keep.tile([P, PASSES * P], U32, align_bytes=64, name="codes_" + name)
+            act_scales[name] = keep.tile([P, PASSES * P], U8, align_bytes=64, name="scales_" + name)
+            nc.vector.quantize_mx(out=act_codes[name][:].bitcast(FP8X4), scales=act_scales[name][:], in_=act_grouped[:])
+
+        spread_vector(0)
 
         pre = {}
         normed = {}
@@ -139,19 +165,10 @@ def tile_layernormlstmcell_pb_kernel(
         def squash(a, cols):
             nc.scalar.activation(out=gate[a][:, cols], in_=normed[a][:, cols], func=ACT.Sigmoid)
 
-        weights = {"f": (Wf_w, Uf_w), "o": (Wo_w, Uo_w)}
-        raw_of = {}
         grouped_of = {}
         codes_of = {}
         scales_of = {}
         sums_of = {}
-
-        def load(i):
-            a = "f" if i < UNITS_PER_GATE else "o"
-            block, which = divmod(i % UNITS_PER_GATE, 2)
-            rows = weights[a][which][block * BLOCK : (block + 1) * BLOCK, :]
-            raw_of[i] = raw_pool.tile([P, ROWS_EACH, WIDTH], BF16, name="raw", tag="raw")
-            nc.sync.dma_start(out=raw_of[i][:], in_=rows.rearrange("(j s) k -> j s k", s=ROWS_EACH))
 
         def transpose_and_copy(i):
             raw_words = raw_of[i][:].bitcast(F32)
@@ -175,13 +192,7 @@ def tile_layernormlstmcell_pb_kernel(
         def quantise(i):
             codes_of[i] = packed_pool.tile([P, PASSES * BLOCK], U32, align_bytes=64, name="codes", tag="codes")
             scales_of[i] = packed_pool.tile([P, PASSES * BLOCK], U8, align_bytes=64, name="scales", tag="scales")
-            for half in range(2):
-                words = slice(half * 2 * BLOCK, (half + 1) * 2 * BLOCK)
-                nc.vector.quantize_mx(
-                    out=codes_of[i][:, words].bitcast(FP8X4),
-                    scales=scales_of[i][:, words],
-                    in_=grouped_of[i][:, half * 8 * BLOCK : (half + 1) * 8 * BLOCK],
-                )
+            nc.vector.quantize_mx(out=codes_of[i][:].bitcast(FP8X4), scales=scales_of[i][:], in_=grouped_of[i][:])
 
         def multiply(i):
             bank_number, place = divmod(i, UNITS_PER_BANK)
@@ -217,50 +228,59 @@ def tile_layernormlstmcell_pb_kernel(
             nc.vector.tensor_scalar_add(out=var_eps[a][:], in0=mean_var[a][:, 1:2], scalar1=EPS)
             nc.gpsimd.tensor_tensor(out=rstd[a][:], in0=var_eps[a][:], in1=minus_half[:], op=ALU.pow)
 
+        STEPS = 4 * CHUNKS
+
         def forget_step_on_vector(step_number):
-            chunk, step = divmod(step_number, 4)
+            chunk, second = divmod(step_number % (2 * CHUNKS), 2)
             cols = chunk_columns(chunk)
-            if step == 0:
-                centre_and_gain("f", cols)
-            if step == 1:
-                scale_and_shift("f", cols)
-            if step == 2:
-                nc.vector.tensor_mul(out=c_new[:, cols], in0=gate["f"][:, cols], in1=c_old[:, cols])
-            if step == 3:
-                nc.vector.tensor_add(out=c_new[:, cols], in0=c_new[:, cols], in1=ic_in[:, cols])
+            if step_number < 2 * CHUNKS:
+                if not second:
+                    centre_and_gain("f", cols)
+                else:
+                    scale_and_shift("f", cols)
+            else:
+                if not second:
+                    nc.vector.tensor_mul(out=c_new[:, cols], in0=gate["f"][:, cols], in1=c_old[:, cols])
+                else:
+                    nc.vector.tensor_add(out=c_new[:, cols], in0=c_new[:, cols], in1=ic_in[:, cols])
 
         def forget_step_on_scalar(step_number):
-            chunk, step = divmod(step_number, 4)
+            chunk, second = divmod(step_number % (2 * CHUNKS), 2)
             cols = chunk_columns(chunk)
-            if step == 1:
+            if second and step_number < 2 * CHUNKS:
                 squash("f", cols)
-            if step == 3:
+            if second and step_number >= 2 * CHUNKS:
                 nc.scalar.activation(out=tanh_c[:, cols], in_=c_new[:, cols], func=ACT.Tanh)
 
-        first_forget_step = UNITS_PER_GATE + LAG
-        for run_start in range(0, UNITS + LAG, UNITS_PER_RUN):
+        first_step_unit = UNITS_PER_GATE + LAG
+        for run_start in range(0, UNITS + LAG + 1, UNITS_PER_RUN):
             run = range(run_start, run_start + UNITS_PER_RUN)
             for i in run:
-                if i == UNITS_PER_GATE:
+                if i == PREFETCH:
+                    for r in range(3, 6):
+                        load_vector(nc.sync, r)
+                if i + PREFETCH == UNITS_PER_GATE:
                     nc.sync.dma_start(out=c_old[:], in_=c)
                     nc.sync.dma_start(out=ic_in[:], in_=ic_tilde)
-                if i < UNITS:
-                    load(i)
+                if i + PREFETCH < UNITS:
+                    load(i + PREFETCH)
                 if 1 <= i <= UNITS:
                     quantise(i - 1)
-                if i >= first_forget_step:
-                    forget_step_on_vector(i - first_forget_step)
+                if 0 <= i - first_step_unit < STEPS:
+                    forget_step_on_vector(i - first_step_unit)
                 if i < UNITS:
                     transpose_and_copy(i)
-                if i >= first_forget_step:
-                    forget_step_on_scalar(i - first_forget_step)
+                if 0 <= i - first_step_unit - 1 < STEPS:
+                    forget_step_on_scalar(i - first_step_unit - 1)
             for i in run:
-                if i >= LAG:
+                if LAG <= i < UNITS + LAG:
                     multiply(i - LAG)
                     if (i - LAG) % UNITS_PER_BANK == UNITS_PER_BANK - 1:
                         add_bias_and_count((i - LAG) // UNITS_PER_BANK)
                     if i - LAG == UNITS_PER_GATE - 1:
                         mean_and_rstd("f")
+            if run_start // UNITS_PER_RUN + 1 < len(vector_names):
+                spread_vector(run_start // UNITS_PER_RUN + 1)
 
         nc.sync.dma_start(out=out_1, in_=c_new[:])
 

@@ -25,7 +25,7 @@ UNITS = 2 * UNITS_PER_GATE
 UNITS_PER_BANK = 2 * BANK // BLOCK
 EPS = 1e-5
 
-UNITS_PER_RUN = 2
+UNITS_PER_RUN = 1
 LAG = 2
 VECTOR_SHARE = 8
 PREFETCH = 3
@@ -125,6 +125,8 @@ def tile_layernormlstmcell_pb_kernel(
             nc.vector.quantize_mx(out=act_codes[name][:].bitcast(FP8X4), scales=act_scales[name][:], in_=act_grouped[:])
 
         spread_vector(0)
+        for r in range(3, 6):
+            load_vector(nc.sync, r)
 
         pre = {}
         normed = {}
@@ -256,9 +258,6 @@ def tile_layernormlstmcell_pb_kernel(
         for run_start in range(0, UNITS + LAG + 1, UNITS_PER_RUN):
             run = range(run_start, run_start + UNITS_PER_RUN)
             for i in run:
-                if i == PREFETCH:
-                    for r in range(3, 6):
-                        load_vector(nc.sync, r)
                 if i + PREFETCH == UNITS_PER_GATE:
                     nc.sync.dma_start(out=c_old[:], in_=c)
                     nc.sync.dma_start(out=ic_in[:], in_=ic_tilde)

from contextlib import ExitStack

import concourse.mybir as mybir
from concourse.masks import make_identity

F32 = mybir.dt.float32
BF16 = mybir.dt.bfloat16
U32 = mybir.dt.uint32
U8 = mybir.dt.uint8
I32 = mybir.dt.int32
FP8X4 = mybir.dt.float8_e4m3fn_x4
ALU = mybir.AluOpType
ACT = mybir.ActivationFunctionType

P = 128
WIDTH = 2048
K_PASS = 512
PASSES = WIDTH // K_PASS
BLOCK = 256
ROWS_EACH = BLOCK // P
BANK = 512
CHUNKS = WIDTH // BANK
UNITS_PER_GATE = 2 * WIDTH // BLOCK
UNITS = 2 * UNITS_PER_GATE
UNITS_PER_BANK = 2 * BANK // BLOCK
EPS = 1e-5

UNITS_PER_RUN = 1
LAG = 2
VECTOR_SHARE = 8
PREFETCH = 3

FLOPS = 2 * P * (2 * WIDTH) * (2 * WIDTH)


def tile_layernormlstmcell_pb_kernel(
    tc, x, h, c, ic_tilde, Wf_w, Wf_b, Uf_w, lnf_g, lnf_b, Wo_w, Wo_b, Uo_w, lno_g, lno_b, out_0, out_1
):
    nc = tc.nc
    with ExitStack() as ctx:
        ctx.enter_context(tc.manual_schedule())
        keep = ctx.enter_context(tc.tile_pool(name="keep", bufs=1))
        stage = ctx.enter_context(tc.tile_pool(name="stage", bufs=2))
        raw_pool = ctx.enter_context(tc.tile_pool(name="raw", bufs=6))
        grouped_pool = ctx.enter_context(tc.tile_pool(name="grouped", bufs=3))
        packed_pool = ctx.enter_context(tc.tile_pool(name="packed", bufs=LAG + UNITS_PER_RUN + 1))
        flip_psum = ctx.enter_context(tc.psum_pool(name="flip", bufs=6))
        sum_psum = ctx.enter_context(tc.psum_pool(name="sums", bufs=2))

        ident_f32 = keep.tile([P, P], F32)
        make_identity(nc, ident_f32[:])
        ident_bf16 = keep.tile([P, P], BF16)
        make_identity(nc, ident_bf16[:])
        minus_half = keep.tile([P, 1], F32)
        nc.vector.memset(minus_half[:], -0.5)

        vectors = {"f_bias": Wf_b, "f_gain": lnf_g, "f_shift": lnf_b, "o_bias": Wo_b, "o_gain": lno_g, "o_shift": lno_b}
        vector_names = list(vectors)
        vector_rows = keep.tile([P, WIDTH], BF16)
        nc.vector.memset(vector_rows[:].bitcast(I32), 0)

        def load_vector(queue, r):
            queue.dma_start(out=vector_rows[r : r + 1, :], in_=vectors[vector_names[r]].rearrange("(o n) -> o n", o=1))

        for r in range(3):
            load_vector(nc.scalar, r)
        table_warm = keep.tile([P, 1], F32)
        nc.scalar.activation(out=table_warm[:], in_=minus_half[:], func=ACT.Sigmoid)

        spread = {}

        def spread_vector(r):
            name = vector_names[r]
            spread[name] = keep.tile([P, WIDTH], BF16, name="spread_" + name)
            for half in range(2):
                copies = flip_psum.tile([P, 2 * BANK], BF16, tag="flip")
                for q in range(2):
                    first = (2 * half + q) * BANK
                    nc.tensor.matmul(
                        out=copies[:, q * BANK : (q + 1) * BANK],
                        lhsT=ident_bf16[:, r : r + 1].to_broadcast([P, P]),
                        rhs=vector_rows[:, first : first + BANK],
                        start=True,
                        stop=True,
                    )
                copy_out = nc.scalar.copy if half == 0 else nc.vector.tensor_copy
                copy_out(out=spread[name][:, half * 2 * BANK : (half + 1) * 2 * BANK], in_=copies[:])

        weights = {"f": (Wf_w, Uf_w), "o": (Wo_w, Uo_w)}
        raw_of = {}

        def load(i):
            a = "f" if i < UNITS_PER_GATE else "o"
            block, which = divmod(i % UNITS_PER_GATE, 2)
            rows = weights[a][which][block * BLOCK : (block + 1) * BLOCK, :]
            raw_of[i] = raw_pool.tile([P, ROWS_EACH, WIDTH], BF16, name="raw", tag="raw")
            nc.sync.dma_start(out=raw_of[i][:], in_=rows.rearrange("(j s) k -> j s k", s=ROWS_EACH))

        act_raw = {}
        for name, source in (("x", x), ("h", h)):
            act_raw[name] = keep.tile([P, WIDTH], BF16, name="raw_" + name)
            nc.sync.dma_start(out=act_raw[name][:], in_=source)
        for i in range(PREFETCH):
            load(i)

        act_codes = {}
        act_scales = {}
        for name in ("x", "h"):
            act_words = act_raw[name][:].bitcast(F32)
            act_grouped = stage.tile([P, PASSES * P * 4], BF16, align_bytes=64)
            act_grouped_words = act_grouped[:].bitcast(F32)
            for pair in range(PASSES // 2):
                flipped = flip_psum.tile([P, 2, 2, P], F32, tag="flip")
                for g in (2 * pair, 2 * pair + 1):
                    for u in range(2):
                        first_word = (2 * g + u) * P
                        nc.tensor.transpose(flipped[:, g % 2, u, :], act_words[:, first_word : first_word + P], ident_f32[:])
                copy_out = nc.scalar.copy if pair == 0 else nc.vector.tensor_copy
                copy_out(
                    out=act_grouped_words[:, pair * BANK : (pair + 1) * BANK].rearrange("p (g b u) -> p g b u", g=2, u=2),
                    in_=flipped[:].rearrange("p g u b -> p g b u"),
                )
            act_codes[name] = keep.tile([P, PASSES * P], U32, align_bytes=64, name="codes_" + name)
            act_scales[name] = keep.tile([P, PASSES * P], U8, align_bytes=64, name="scales_" + name)
            nc.vector.quantize_mx(out=act_codes[name][:].bitcast(FP8X4), scales=act_scales[name][:], in_=act_grouped[:])

        spread_vector(0)
        for r in range(3, 6):
            load_vector(nc.sync, r)

        pre = {}
        normed = {}
        gate = {}
        stats = {}
        mean_var = {}
        var_eps = {}
        rstd = {}
        for a in ("f", "o"):
            pre[a] = keep.tile([P, WIDTH], F32, name="pre_" + a)
            normed[a] = keep.tile([P, WIDTH], F32, name="normed_" + a)
            gate[a] = keep.tile([P, WIDTH], F32, name="gate_" + a)
            stats[a] = keep.tile([P, CHUNKS, 6], F32, name="stats_" + a)
            mean_var[a] = keep.tile([P, 2], F32, name="mean_var_" + a)
            var_eps[a] = keep.tile([P, 1], F32, name="var_eps_" + a)
            rstd[a] = keep.tile([P, 1], F32, name="rstd_" + a)
        c_old = keep.tile([P, WIDTH], BF16)
        ic_in = keep.tile([P, WIDTH], BF16)
        c_new = keep.tile([P, WIDTH], F32)
        tanh_c = keep.tile([P, WIDTH], F32)
        h_new = keep.tile([P, WIDTH], F32)

        def chunk_columns(chunk):
            return slice(chunk * BANK, (chunk + 1) * BANK)

        def centre_and_gain(a, cols):
            nc.vector.scalar_tensor_tensor(
                out=normed[a][:, cols], in0=pre[a][:, cols], scalar=mean_var[a][:, 0:1],
                in1=spread[a + "_gain"][:, cols], op0=ALU.subtract, op1=ALU.mult,
            )

        def scale_and_shift(a, cols):
            nc.vector.scalar_tensor_tensor(
                out=normed[a][:, cols], in0=normed[a][:, cols], scalar=rstd[a][:, 0:1],
                in1=spread[a + "_shift"][:, cols], op0=ALU.mult, op1=ALU.add,
            )

        def squash(a, cols):
            nc.scalar.activation(out=gate[a][:, cols], in_=normed[a][:, cols], func=ACT.Sigmoid)

        grouped_of = {}
        codes_of = {}
        scales_of = {}
        sums_of = {}

        def transpose_and_copy(i):
            raw_words = raw_of[i][:].bitcast(F32)
            grouped_of[i] = grouped_pool.tile([P, PASSES * BLOCK * 4], BF16, align_bytes=64, name="grouped", tag="grouped")
            grouped_words = grouped_of[i][:].bitcast(F32)
            for g in range(PASSES):
                flipped = flip_psum.tile([P, 2, BLOCK], F32, tag="flip")
                for u in range(2):
                    for s in range(ROWS_EACH):
                        first_word = (2 * g + u) * P
                        nc.tensor.transpose(
                            flipped[:, u, s * P : (s + 1) * P], raw_words[:, s, first_word : first_word + P], ident_f32[:]
                        )
                to_vector = (PASSES * i + g) % VECTOR_SHARE == VECTOR_SHARE - 1
                copy_out = nc.vector.tensor_copy if to_vector else nc.scalar.copy
                copy_out(
                    out=grouped_words[:, g * BANK : (g + 1) * BANK].rearrange("p (n u) -> p n u", u=2),
                    in_=flipped[:].rearrange("p u n -> p n u"),
                )

        def quantise(i):
            codes_of[i] = packed_pool.tile([P, PASSES * BLOCK], U32, align_bytes=64, name="codes", tag="codes")
            scales_of[i] = packed_pool.tile([P, PASSES * BLOCK], U8, align_bytes=64, name="scales", tag="scales")
            nc.vector.quantize_mx(out=codes_of[i][:].bitcast(FP8X4), scales=scales_of[i][:], in_=grouped_of[i][:])

        def multiply(i):
            bank_number, place = divmod(i, UNITS_PER_BANK)
            block_in_bank, which = divmod(place, 2)
            if place == 0:
                sums_of[bank_number] = sum_psum.tile([P, BANK], F32, name="sums", tag="sums")
            name = "x" if which == 0 else "h"
            for g in range(PASSES):
                nc.tensor.matmul_mx(
                    out=sums_of[bank_number][:, block_in_bank * BLOCK : (block_in_bank + 1) * BLOCK],
                    lhsT=act_codes[name][:, g * P : (g + 1) * P].bitcast(FP8X4),
                    lhsT_scale=act_scales[name][:, g * P : (g + 1) * P],
                    rhs=codes_of[i][:, g * BLOCK : (g + 1) * BLOCK].bitcast(FP8X4),
                    rhs_scale=scales_of[i][:, g * BLOCK : (g + 1) * BLOCK],
                    start=(which == 0 and g == 0),
                    stop=(which == 1 and g == PASSES - 1),
                )

        def add_bias_and_count(bank_number):
            a = "f" if bank_number < CHUNKS else "o"
            chunk = bank_number % CHUNKS
            cols = chunk_columns(chunk)
            nc.vector.tensor_tensor(
                out=pre[a][:, cols].rearrange("p (b j s) -> p b j s", b=2, s=ROWS_EACH),
                in0=sums_of[bank_number][:].rearrange("p (b s j) -> p b j s", b=2, s=ROWS_EACH),
                in1=spread[a + "_bias"][:, cols].rearrange("p (b j s) -> p b j s", b=2, s=ROWS_EACH),
                op=ALU.add,
            )
            nc.vector.bn_stats(out=stats[a][:, chunk, :], in_=pre[a][:, cols])

        def mean_and_rstd(a):
            nc.vector.bn_aggr(out=mean_var[a][:], in_=stats[a][:].rearrange("p n six -> p (n six)"))
            nc.vector.tensor_scalar_add(out=var_eps[a][:], in0=mean_var[a][:, 1:2], scalar1=EPS)
            nc.gpsimd.tensor_tensor(out=rstd[a][:], in0=var_eps[a][:], in1=minus_half[:], op=ALU.pow)

        STEPS = 4 * CHUNKS

        def forget_step_on_vector(step_number):
            chunk, second = divmod(step_number % (2 * CHUNKS), 2)
            cols = chunk_columns(chunk)
            if step_number < 2 * CHUNKS:
                if not second:
                    centre_and_gain("f", cols)
                else:
                    scale_and_shift("f", cols)
            else:
                if not second:
                    nc.vector.tensor_mul(out=c_new[:, cols], in0=gate["f"][:, cols], in1=c_old[:, cols])
                else:
                    nc.vector.tensor_add(out=c_new[:, cols], in0=c_new[:, cols], in1=ic_in[:, cols])

        def forget_step_on_scalar(step_number):
            chunk, second = divmod(step_number % (2 * CHUNKS), 2)
            cols = chunk_columns(chunk)
            if second and step_number < 2 * CHUNKS:
                squash("f", cols)
            if second and step_number >= 2 * CHUNKS:
                nc.scalar.activation(out=tanh_c[:, cols], in_=c_new[:, cols], func=ACT.Tanh)

        first_step_unit = UNITS_PER_GATE + LAG
        for run_start in range(0, UNITS + LAG + 1, UNITS_PER_RUN):
            run = range(run_start, run_start + UNITS_PER_RUN)
            for i in run:
                if i + PREFETCH == UNITS_PER_GATE:
                    nc.sync.dma_start(out=c_old[:], in_=c)
                    nc.sync.dma_start(out=ic_in[:], in_=ic_tilde)
                if i + PREFETCH < UNITS:
                    load(i + PREFETCH)
                if 1 <= i <= UNITS:
                    quantise(i - 1)
                if 0 <= i - first_step_unit < STEPS:
                    forget_step_on_vector(i - first_step_unit)
                if i < UNITS:
                    transpose_and_copy(i)
                if 0 <= i - first_step_unit - 1 < STEPS:
                    forget_step_on_scalar(i - first_step_unit - 1)
            for i in run:
                if LAG <= i < UNITS + LAG:
                    multiply(i - LAG)
                    if (i - LAG) % UNITS_PER_BANK == UNITS_PER_BANK - 1:
                        add_bias_and_count((i - LAG) // UNITS_PER_BANK)
                    if i - LAG == UNITS_PER_GATE - 1:
                        mean_and_rstd("f")
            if run_start // UNITS_PER_RUN + 1 < len(vector_names):
                spread_vector(run_start // UNITS_PER_RUN + 1)

        nc.sync.dma_start(out=out_1, in_=c_new[:])

        mean_and_rstd("o")
        for chunk in range(CHUNKS):
            centre_and_gain("o", chunk_columns(chunk))
        for chunk in range(CHUNKS):
            scale_and_shift("o", chunk_columns(chunk))
            squash("o", chunk_columns(chunk))
        for chunk in range(CHUNKS):
            cols = chunk_columns(chunk)
            nc.vector.tensor_mul(out=h_new[:, cols], in0=gate["o"][:, cols], in1=tanh_c[:, cols])
            nc.sync.dma_start(out=out_0[:, cols], in_=h_new[:, cols])
